import numpy as np
import ml_dtypes


def mxq(x, axis, fmt="e4m3"):
    dtype, down = {"e4m3": (ml_dtypes.float8_e4m3fn, 7), "e5m2": (ml_dtypes.float8_e5m2, 14)}[fmt]
    v = np.moveaxis(np.asarray(x, np.float32).astype(ml_dtypes.bfloat16).astype(np.float64), axis, -1)
    blocks = v.reshape(v.shape[:-1] + (-1, 32))
    amax = np.abs(blocks).max(-1, keepdims=True)
    byte = np.maximum(np.where(amax > 0, np.frexp(amax)[1] - 1 + 127, 0) - down, 1)
    scale = np.exp2(byte - 127.0)
    codes = (blocks / scale).astype(np.float32).astype(dtype).astype(np.float64)
    return np.moveaxis((codes * scale).reshape(v.shape), -1, axis)


WIDE = False


def mx_kscale(k):
    if not WIDE:
        return np.ones(k)
    levels = np.array([10, -10, 5, -5, 0])
    if k % 512:
        return np.exp2(np.random.permutation(np.resize(levels, k // 32))).repeat(32)
    a = np.empty((k // 512, 16))
    for p in range(k // 512):
        a[p, :8] = np.random.permutation(np.resize(levels, 8))
        for g in range(8):
            far = levels[np.abs(levels - a[p, g]) >= 10]
            a[p, g + 8] = far[np.random.randint(len(far))]
    return np.exp2(a.ravel()).repeat(32)


BF16 = ml_dtypes.bfloat16


def bf(x):
    return np.asarray(x, np.float32).astype(BF16)


def f64(x):
    return np.asarray(x).astype(np.float64)


N, NQ, G, KW = 256, 1024, 3, 3
P = KW - 1


def x_taps(x):
    return np.moveaxis(x.reshape(N, NQ, G, P), -1, 0).swapaxes(-1, -2).reshape(P, N * G, NQ)


def q_rows(q):
    return q.swapaxes(-1, -2).reshape(N * G, NQ)


def conv(xq, qq, W, b):
    wt = W.transpose(2, 1, 0)
    return (xq @ mxq(wt[:P], 1, "e4m3")).sum(0) + (qq @ mxq(wt[P], 0, "e4m3")) + b


def setup_inputs():
    s = mx_kscale(NQ)
    w = 1.0 / np.sqrt(KW * NQ)
    return {"x": bf(np.random.standard_normal((N, NQ, G * P)) * s[None, :, None]),
            "q2": bf(np.maximum(np.random.standard_normal((N, NQ, G)) * 0.9, 0.0) * s[None, :, None]),
            "q1": bf(np.random.standard_normal((N, NQ, G))),
            "W3": bf(np.random.standard_normal((NQ, NQ, KW)) * w / s[None, :, None]),
            "b3": bf(np.random.standard_normal(NQ) * 0.2)}


def reference(x, q2, q1, W3, b3):
    y = conv(mxq(x_taps(f64(x)), 2, "e4m3"), mxq(q_rows(f64(q2)), 1, "e4m3"), f64(W3), f64(b3))
    return np.maximum(y.reshape(N, G, NQ).swapaxes(-1, -2) + f64(q1), 0.0)

@@ -1,0 +1,212 @@
+from contextlib import ExitStack
+
+import concourse.mybir as mybir
+from concourse.masks import make_identity
+
+FP8X4 = mybir.dt.float8_e4m3fn_x4
+BF16 = mybir.dt.bfloat16
+F32 = mybir.dt.float32
+U32 = mybir.dt.uint32
+U8 = mybir.dt.uint8
+ADD = mybir.AluOpType.add
+RELU = mybir.ActivationFunctionType.Relu
+
+P = 128
+N_ROWS, CHANNELS, GROUPS, TAPS = 256, 1024, 3, 3
+ROW_TILES = N_ROWS // P
+W_TILES = CHANNELS // P
+K_PASS = 512
+HALVES = CHANNELS // K_PASS
+SIXTHS = 6
+UNIT = SIXTHS * K_PASS
+BANKS = 3
+FLOPS = 2 * N_ROWS * GROUPS * CHANNELS * CHANNELS * TAPS
+
+UNITS = (
+    [("q2", i, 0) for i in range(ROW_TILES)]
+    + [("x", i, h) for i in range(ROW_TILES) for h in range(HALVES)]
+    + [("w", j, 0) for j in range(W_TILES)]
+)
+FIRST_W = len(UNITS) - W_TILES
+LOADS_BEFORE_RESIDUAL = FIRST_W + 2
+VECTOR_COLS = 416
+COPY_BUFS = 3
+GROUPED_BUFS = 3
+TRANSPOSE_BANKS = 4
+PRODUCT_BANKS = 4
+
+
+def tile_quadjetresnetblock_pb_kernel(tc, x, q2, q1, W3, b3, out):
+    nc = tc.nc
+    with ExitStack() as ctx:
+        ctx.enter_context(tc.manual_schedule())
+        fixed = ctx.enter_context(tc.tile_pool(name="fixed", bufs=1))
+        rotating = ctx.enter_context(tc.tile_pool(name="rotating", bufs=1))
+        psum = ctx.enter_context(tc.psum_pool(name="psum", bufs=1))
+
+        identity = fixed.tile([P, P], F32, name="identity")
+        make_identity(nc, identity[:])
+        bias = fixed.tile([P, CHANNELS], BF16, name="bias")
+        loaded, codes, scales = {}, {}, {}
+        for unit in UNITS:
+            loaded[unit] = fixed.tile([P, UNIT], BF16, name="loaded_%s%d%d" % unit)
+            codes[unit] = fixed.tile([P, UNIT // 4], U32, name="codes_%s%d%d" % unit, align_bytes=64)
+            scales[unit] = fixed.tile([P, UNIT // 4], U8, name="scales_%s%d%d" % unit, align_bytes=64)
+        q1_loaded = fixed.tile([P, ROW_TILES, GROUPS * CHANNELS], BF16, name="q1_loaded")
+        result = [fixed.tile([P, ROW_TILES, GROUPS * P], F32, name="result%d" % j) for j in range(W_TILES)]
+
+        def rows(i):
+            return slice(P * i, P * (i + 1))
+
+        for k, unit in enumerate(UNITS):
+            kind, i, h = unit
+            if k == LOADS_BEFORE_RESIDUAL:
+                nc.sync.dma_start(out=bias[:], in_=b3.partition_broadcast(P))
+                for r in range(ROW_TILES):
+                    nc.sync.dma_start(out=q1_loaded[:, r, :], in_=q1[rows(r), :, :].rearrange("n o g -> n (o g)"))
+            if kind == "x":
+                source = x[rows(i), K_PASS * h:K_PASS * (h + 1), :].rearrange("n c j -> n (c j)")
+            elif kind == "q2":
+                source = q2[rows(i), :, :].rearrange("n c g -> n (c g)")
+            else:
+                source = W3[rows(i), :, :].rearrange("o c t -> o (c t)")
+            if k == 0:
+                for half in range(HALVES):
+                    cols = slice(UNIT // 2 * half, UNIT // 2 * (half + 1))
+                    nc.sync.dma_start(out=loaded[unit][:, cols], in_=source[:, cols])
+            else:
+                nc.sync.dma_start(out=loaded[unit][:], in_=source)
+
+        apart, transposed, grouped, product = {}, {}, {}, {}
+
+        def copy(on_vector, dst, src):
+            if on_vector:
+                nc.vector.tensor_copy(out=dst, in_=src)
+            else:
+                nc.scalar.copy(out=dst, in_=src)
+
+        def set_taps_apart(k):
+            unit = UNITS[k]
+            if unit[0] == "x":
+                return
+            tag = "apart%d" % (k % COPY_BUFS)
+            apart[k] = rotating.tile([P, SIXTHS, K_PASS], BF16, name=tag, tag=tag)
+            src = loaded[unit][:].rearrange("p (j s) -> p s j", s=SIXTHS)
+            parts = HALVES if k == 0 else 1
+            for part in range(parts):
+                start, width = K_PASS // parts * part, K_PASS // parts
+                cut = start + VECTOR_COLS // parts
+                for on_vector, lo, hi in ((True, start, cut), (False, cut, start + width)):
+                    copy(on_vector, apart[k][:, :, lo:hi], src[:, :, lo:hi])
+
+        def transpose(k):
+            unit = UNITS[k]
+            transposed[k] = []
+            for b in range(BANKS):
+                tag = "transposed%d" % ((BANKS * k + b) % TRANSPOSE_BANKS)
+                bank = psum.tile([P, 4, P], F32, name=tag, tag=tag)
+                transposed[k].append(bank)
+                if unit[0] == "x":
+                    words = loaded[unit][:].bitcast(F32).rearrange("r (p e u g) -> r u e g p", e=2, u=2, g=GROUPS)
+                    for u in range(2):
+                        for e in range(2):
+                            nc.tensor.transpose(bank[:, 2 * u + e, :], words[:, u, e, b, :], identity[:])
+                else:
+                    for h in range(HALVES):
+                        for u in range(2):
+                            run = apart[k][:, TAPS * u + b, 256 * h:256 * (h + 1)]
+                            nc.tensor.transpose(bank[:, 2 * h + u, :], run.bitcast(F32), identity[:])
+
+        def regroup(k):
+            unit = UNITS[k]
+            tag = "grouped%d" % (k % GROUPED_BUFS)
+            grouped[k] = rotating.tile([P, UNIT // 2], F32, name=tag, tag=tag, align_bytes=64)
+            for b in range(BANKS):
+                dst = grouped[k][:, 512 * b:512 * (b + 1)]
+                bank = transposed[k][b][:]
+                if unit[0] == "x":
+                    copy(
+                        b == BANKS - 1,
+                        dst.bitcast(BF16).rearrange("p (t r v) -> p t r v", t=2, v=4),
+                        bank.bitcast(BF16).rearrange("p v (r t) -> p t r v", t=2),
+                    )
+                else:
+                    copy(
+                        False,
+                        dst.rearrange("p (h r u) -> p h r u", h=2, u=2),
+                        bank.rearrange("p (h u) r -> p h r u", u=2),
+                    )
+
+        def quantise(k):
+            unit = UNITS[k]
+            for lo, hi in ((0, 512), (512, 768)):
+                nc.vector.quantize_mx(
+                    out=codes[unit][:, lo:hi].bitcast(FP8X4),
+                    scales=scales[unit][:, lo:hi],
+                    in_=grouped[k][:, 2 * lo:2 * hi].bitcast(BF16),
+                )
+
+        def operand(unit, sixth):
+            cols = slice(P * sixth, P * (sixth + 1))
+            return codes[unit][:, cols].bitcast(FP8X4), scales[unit][:, cols]
+
+        def multiply(i, j):
+            tag = "product%d" % ((ROW_TILES * j + i) % PRODUCT_BANKS)
+            product[(i, j)] = psum.tile([P, GROUPS, P], F32, name=tag, tag=tag)
+            passes = [(t, h) for t in range(TAPS) for h in range(HALVES)]
+            for g in range(GROUPS):
+                for t, h in passes:
+                    if t < 2:
+                        a_codes, a_scales = operand(("x", i, h), 2 * g + t)
+                    else:
+                        a_codes, a_scales = operand(("q2", i, 0), HALVES * g + h)
+                    w_codes, w_scales = operand(("w", j, 0), HALVES * t + h)
+                    nc.tensor.matmul_mx(
+                        out=product[(i, j)][:, g, :],
+                        lhsT=a_codes,
+                        lhsT_scale=a_scales,
+                        rhs=w_codes,
+                        rhs_scale=w_scales,
+                        start=(t, h) == passes[0],
+                        stop=(t, h) == passes[-1],
+                    )
+
+        def residual_plus_bias(j):
+            nc.vector.tensor_tensor(
+                out=result[j][:].rearrange("p i (o g) -> p i o g", g=GROUPS),
+                in0=q1_loaded[:, :, GROUPS * P * j:GROUPS * P * (j + 1)].rearrange("p i (o g) -> p i o g", g=GROUPS),
+                in1=bias[:, P * j:P * (j + 1)].unsqueeze(1).unsqueeze(3).to_broadcast([P, ROW_TILES, P, GROUPS]),
+                op=ADD,
+            )
+
+        def add_product(i, j):
+            view = result[j][:, i, :].rearrange("p (o g) -> p o g", g=GROUPS)
+            nc.vector.tensor_tensor(out=view, in0=product[(i, j)][:].rearrange("p g o -> p o g"), in1=view, op=ADD)
+
+        def relu_and_store(i, j):
+            nc.scalar.activation(out=result[j][:, i, :], in_=result[j][:, i, :], func=RELU)
+            nc.sync.dma_start(
+                out=out[rows(i), P * j:P * (j + 1), :].rearrange("n o g -> n (o g)"), in_=result[j][:, i, :]
+            )
+
+        for step in range(len(UNITS) + 3):
+            multiplied = step - 2 - FIRST_W
+            finished = multiplied - 1
+            if 0 <= step - 2 < len(UNITS):
+                quantise(step - 2)
+            if 0 <= finished < W_TILES:
+                for i in range(ROW_TILES):
+                    add_product(i, finished)
+            if step < len(UNITS):
+                set_taps_apart(step)
+            if 0 <= step - 1 < len(UNITS):
+                transpose(step - 1)
+            if 0 <= multiplied < W_TILES:
+                for i in range(ROW_TILES):
+                    multiply(i, multiplied)
+                residual_plus_bias(multiplied)
+            if 0 <= step - 1 < len(UNITS):
+                regroup(step - 1)
+            if 0 <= finished < W_TILES:
+                for i in range(ROW_TILES):
+                    relu_and_store(i, finished)

@@ -91,13 +91,14 @@ def tile_quadjetresnetblock_pb_kernel(tc, x, q2, q1, W3, b3, out):
                 return
             tag = "apart%d" % (k % COPY_BUFS)
             apart[k] = rotating.tile([P, SIXTHS, K_PASS], BF16, name=tag, tag=tag)
-            src = loaded[unit][:].rearrange("p (j s) -> p s j", s=SIXTHS)
+            src = loaded[unit][:].rearrange("p (m u e t) -> p t m u e", u=2, e=2, t=TAPS)
+            dst = apart[k][:].rearrange("p (t u) (m e) -> p t m u e", u=2, e=2)
             parts = HALVES if k == 0 else 1
             for part in range(parts):
                 start, width = K_PASS // parts * part, K_PASS // parts
                 cut = start + VECTOR_COLS // parts
                 for on_vector, lo, hi in ((True, start, cut), (False, cut, start + width)):
-                    copy(on_vector, apart[k][:, :, lo:hi], src[:, :, lo:hi])
+                    copy(on_vector, dst[:, :, lo // 2:hi // 2], src[:, :, lo // 2:hi // 2])
 
         def transpose(k):
             unit = UNITS[k]
@@ -107,14 +108,14 @@ def tile_quadjetresnetblock_pb_kernel(tc, x, q2, q1, W3, b3, out):
                 bank = psum.tile([P, 4, P], F32, name=tag, tag=tag)
                 transposed[k].append(bank)
                 if unit[0] == "x":
-                    words = loaded[unit][:].bitcast(F32).rearrange("r (p e u g) -> r u e g p", e=2, u=2, g=GROUPS)
+                    words = loaded[unit][:].bitcast(F32).rearrange("r (p u e g) -> r u e g p", u=2, e=2, g=GROUPS)
                     for u in range(2):
                         for e in range(2):
                             nc.tensor.transpose(bank[:, 2 * u + e, :], words[:, u, e, b, :], identity[:])
                 else:
                     for h in range(HALVES):
                         for u in range(2):
-                            run = apart[k][:, TAPS * u + b, 256 * h:256 * (h + 1)]
+                            run = apart[k][:, 2 * b + u, 256 * h:256 * (h + 1)]
                             nc.tensor.transpose(bank[:, 2 * h + u, :], run.bitcast(F32), identity[:])
 
         def regroup(k):

@@ -46,6 +46,11 @@ def tile_quadjetresnetblock_pb_kernel(tc, x, q2, q1, W3, b3, out):
 
         identity = fixed.tile([P, P], F32, name="identity")
         make_identity(nc, identity[:])
+        bias_row = fixed.tile([P, CHANNELS], BF16, name="bias_row")
+        nc.vector.memset(bias_row[:], 0.0)
+        ones = fixed.tile([P, P], BF16, name="ones")
+        nc.vector.memset(ones[:], 1.0)
+        nc.sync.dma_start(out=bias_row[0:1, :], in_=b3.rearrange("(a o) -> a o", a=1))
         bias = fixed.tile([P, CHANNELS], BF16, name="bias")
         loaded, codes, scales = {}, {}, {}
         for unit in UNITS:
@@ -61,7 +66,6 @@ def tile_quadjetresnetblock_pb_kernel(tc, x, q2, q1, W3, b3, out):
         for k, unit in enumerate(UNITS):
             kind, i, h = unit
             if k == LOADS_BEFORE_RESIDUAL:
-                nc.sync.dma_start(out=bias[:], in_=b3.partition_broadcast(P))
                 for r in range(ROW_TILES):
                     nc.sync.dma_start(out=q1_loaded[:, r, :], in_=q1[rows(r), :, :].rearrange("n o g -> n (o g)"))
             if kind == "x":
@@ -190,6 +194,14 @@ def tile_quadjetresnetblock_pb_kernel(tc, x, q2, q1, W3, b3, out):
                 out=out[rows(i), P * j:P * (j + 1), :].rearrange("n o g -> n (o g)"), in_=result[j][:, i, :]
             )
 
+        def spread_bias():
+            for h in range(HALVES):
+                cols = slice(K_PASS * h, K_PASS * (h + 1))
+                tag = "product%d" % h
+                bank = psum.tile([P, K_PASS], F32, name=tag, tag=tag)
+                nc.tensor.matmul(out=bank[:], lhsT=ones[:], rhs=bias_row[:, cols], start=True, stop=True)
+                nc.vector.tensor_copy(out=bias[:, cols], in_=bank[:])
+
         for step in range(len(UNITS) + 3):
             multiplied = step - 2 - FIRST_W
             finished = multiplied - 1
@@ -200,6 +212,8 @@ def tile_quadjetresnetblock_pb_kernel(tc, x, q2, q1, W3, b3, out):
                     add_product(i, finished)
             if step < len(UNITS):
                 set_taps_apart(step)
+            if step == 0:
+                spread_bias()
             if 0 <= step - 1 < len(UNITS):
                 transpose(step - 1)
             if 0 <= multiplied < W_TILES:

@@ -50,7 +50,6 @@ def tile_quadjetresnetblock_pb_kernel(tc, x, q2, q1, W3, b3, out):
         nc.vector.memset(bias_row[:], 0.0)
         ones = fixed.tile([P, P], BF16, name="ones")
         nc.vector.memset(ones[:], 1.0)
-        nc.sync.dma_start(out=bias_row[0:1, :], in_=b3.rearrange("(a o) -> a o", a=1))
         bias = fixed.tile([P, CHANNELS], BF16, name="bias")
         loaded, codes, scales = {}, {}, {}
         for unit in UNITS:
@@ -78,6 +77,7 @@ def tile_quadjetresnetblock_pb_kernel(tc, x, q2, q1, W3, b3, out):
                 for half in range(HALVES):
                     cols = slice(UNIT // 2 * half, UNIT // 2 * (half + 1))
                     nc.sync.dma_start(out=loaded[unit][:, cols], in_=source[:, cols])
+                nc.sync.dma_start(out=bias_row[0:1, :], in_=b3.rearrange("(a o) -> a o", a=1))
             else:
                 nc.sync.dma_start(out=loaded[unit][:], in_=source)
 
@@ -212,7 +212,7 @@ def tile_quadjetresnetblock_pb_kernel(tc, x, q2, q1, W3, b3, out):
                     add_product(i, finished)
             if step < len(UNITS):
                 set_taps_apart(step)
-            if step == 0:
+            if step == 2:
                 spread_bias()
             if 0 <= step - 1 < len(UNITS):
                 transpose(step - 1)

@@ -24,12 +24,16 @@ FLOPS = 2 * N_ROWS * GROUPS * CHANNELS * CHANNELS * TAPS
 
 UNITS = (
     [("q2", i, 0) for i in range(ROW_TILES)]
-    + [("x", i, h) for i in range(ROW_TILES) for h in range(HALVES)]
-    + [("w", j, 0) for j in range(W_TILES)]
+    + [("x", 0, h) for h in range(HALVES)]
+    + [("w", 0, 0)]
+    + [("x", 1, h) for h in range(HALVES)]
+    + [("w", j, 0) for j in range(1, W_TILES)]
 )
-FIRST_W = len(UNITS) - W_TILES
-LOADS_BEFORE_RESIDUAL = FIRST_W + 2
-VECTOR_COLS = 416
+LOADS_BEFORE_RESIDUAL = 8
+FIRST_RESIDUAL_STEP = 8
+PRODUCTS_A_STEP = 3
+VECTOR_COLS = 384
+LATE_W, LATE_VECTOR_COLS = 4, 288
 COPY_BUFS = 3
 GROUPED_BUFS = 3
 TRANSPOSE_BANKS = 4
@@ -100,7 +104,7 @@ def tile_quadjetresnetblock_pb_kernel(tc, x, q2, q1, W3, b3, out):
             parts = HALVES if k == 0 else 1
             for part in range(parts):
                 start, width = K_PASS // parts * part, K_PASS // parts
-                cut = start + VECTOR_COLS // parts
+                cut = start + (LATE_VECTOR_COLS if unit[0] == "w" and unit[1] >= LATE_W else VECTOR_COLS) // parts
                 for on_vector, lo, hi in ((True, start, cut), (False, cut, start + width)):
                     copy(on_vector, dst[:, :, lo // 2:hi // 2], src[:, :, lo // 2:hi // 2])
 
@@ -131,13 +135,13 @@ def tile_quadjetresnetblock_pb_kernel(tc, x, q2, q1, W3, b3, out):
                 bank = transposed[k][b][:]
                 if unit[0] == "x":
                     copy(
-                        b == BANKS - 1,
+                        b == 1,
                         dst.bitcast(BF16).rearrange("p (t r v) -> p t r v", t=2, v=4),
                         bank.bitcast(BF16).rearrange("p v (r t) -> p t r v", t=2),
                     )
                 else:
                     copy(
-                        False,
+                        k % 2 == 0 and b == BANKS - 1,
                         dst.rearrange("p (h r u) -> p h r u", h=2, u=2),
                         bank.rearrange("p (h u) r -> p h r u", u=2),
                     )
@@ -156,7 +160,7 @@ def tile_quadjetresnetblock_pb_kernel(tc, x, q2, q1, W3, b3, out):
             return codes[unit][:, cols].bitcast(FP8X4), scales[unit][:, cols]
 
         def multiply(i, j):
-            tag = "product%d" % ((ROW_TILES * j + i) % PRODUCT_BANKS)
+            tag = "product%d" % (len(product) % PRODUCT_BANKS)
             product[(i, j)] = psum.tile([P, GROUPS, P], F32, name=tag, tag=tag)
             passes = [(t, h) for t in range(TAPS) for h in range(HALVES)]
             for g in range(GROUPS):
@@ -202,26 +206,33 @@ def tile_quadjetresnetblock_pb_kernel(tc, x, q2, q1, W3, b3, out):
                 nc.tensor.matmul(out=bank[:], lhsT=ones[:], rhs=bias_row[:, cols], start=True, stop=True)
                 nc.vector.tensor_copy(out=bias[:, cols], in_=bank[:])
 
-        for step in range(len(UNITS) + 3):
-            multiplied = step - 2 - FIRST_W
-            finished = multiplied - 1
-            if 0 <= step - 2 < len(UNITS):
-                quantise(step - 2)
-            if 0 <= finished < W_TILES:
-                for i in range(ROW_TILES):
-                    add_product(i, finished)
+        ready, waiting, multiplied, added = set(), [], [], []
+        step = 0
+        while step < len(UNITS) + 2 or waiting or multiplied or added:
             if step < len(UNITS):
                 set_taps_apart(step)
             if step == 2:
                 spread_bias()
             if 0 <= step - 1 < len(UNITS):
                 transpose(step - 1)
-            if 0 <= multiplied < W_TILES:
-                for i in range(ROW_TILES):
-                    multiply(i, multiplied)
-                residual_plus_bias(multiplied)
+            for i, j in added:
+                relu_and_store(i, j)
+            now, waiting = waiting[:PRODUCTS_A_STEP], waiting[PRODUCTS_A_STEP:]
+            for i, j in now:
+                multiply(i, j)
+            if 0 <= step - 2 < len(UNITS):
+                quantise(step - 2)
+                ready.add(UNITS[step - 2])
+                for j in range(W_TILES):
+                    for i in range(ROW_TILES):
+                        needs = {("q2", i, 0), ("x", i, 0), ("x", i, 1), ("w", j, 0)}
+                        if needs <= ready and UNITS[step - 2] in needs:
+                            waiting.append((i, j))
             if 0 <= step - 1 < len(UNITS):
                 regroup(step - 1)
-            if 0 <= finished < W_TILES:
-                for i in range(ROW_TILES):
-                    relu_and_store(i, finished)
+            if 0 <= step - FIRST_RESIDUAL_STEP < W_TILES:
+                residual_plus_bias(step - FIRST_RESIDUAL_STEP)
+            for i, j in multiplied:
+                add_product(i, j)
+            added, multiplied = multiplied, now
+            step += 1

@@ -32,8 +32,8 @@ UNITS = (
 LOADS_BEFORE_RESIDUAL = 8
 FIRST_RESIDUAL_STEP = 8
 PRODUCTS_A_STEP = 3
-VECTOR_COLS = 384
-LATE_W, LATE_VECTOR_COLS = 4, 288
+VECTOR_COLS = 416
+LATE_W, LATE_VECTOR_COLS = 3, 256
 COPY_BUFS = 3
 GROUPED_BUFS = 3
 TRANSPOSE_BANKS = 4
@@ -48,12 +48,12 @@ def tile_quadjetresnetblock_pb_kernel(tc, x, q2, q1, W3, b3, out):
         rotating = ctx.enter_context(tc.tile_pool(name="rotating", bufs=1))
         psum = ctx.enter_context(tc.psum_pool(name="psum", bufs=1))
 
+        bias_row = fixed.tile([P, CHANNELS], BF16, name="bias_row")
+        nc.gpsimd.memset(bias_row[:], 0.0)
+        ones = fixed.tile([P, P], BF16, name="ones")
+        nc.gpsimd.memset(ones[:], 1.0)
         identity = fixed.tile([P, P], F32, name="identity")
         make_identity(nc, identity[:])
-        bias_row = fixed.tile([P, CHANNELS], BF16, name="bias_row")
-        nc.vector.memset(bias_row[:], 0.0)
-        ones = fixed.tile([P, P], BF16, name="ones")
-        nc.vector.memset(ones[:], 1.0)
         bias = fixed.tile([P, CHANNELS], BF16, name="bias")
         loaded, codes, scales = {}, {}, {}
         for unit in UNITS:
@@ -81,7 +81,8 @@ def tile_quadjetresnetblock_pb_kernel(tc, x, q2, q1, W3, b3, out):
                 for half in range(HALVES):
                     cols = slice(UNIT // 2 * half, UNIT // 2 * (half + 1))
                     nc.sync.dma_start(out=loaded[unit][:, cols], in_=source[:, cols])
-                nc.sync.dma_start(out=bias_row[0:1, :], in_=b3.rearrange("(a o) -> a o", a=1))
+                    if half == 0:
+                        nc.sync.dma_start(out=bias_row[0:1, :], in_=b3.rearrange("(a o) -> a o", a=1))
             else:
                 nc.sync.dma_start(out=loaded[unit][:], in_=source)
 
@@ -105,8 +106,11 @@ def tile_quadjetresnetblock_pb_kernel(tc, x, q2, q1, W3, b3, out):
             for part in range(parts):
                 start, width = K_PASS // parts * part, K_PASS // parts
                 cut = start + (LATE_VECTOR_COLS if unit[0] == "w" and unit[1] >= LATE_W else VECTOR_COLS) // parts
-                for on_vector, lo, hi in ((True, start, cut), (False, cut, start + width)):
-                    copy(on_vector, dst[:, :, lo // 2:hi // 2], src[:, :, lo // 2:hi // 2])
+                words = slice(start // 2, cut // 2)
+                copy(True, dst[:, 0:2, words], src[:, 0:2, words])
+                copy(True, dst[:, 2, words], src[:, 2, words])
+                words = slice(cut // 2, (start + width) // 2)
+                copy(False, dst[:, :, words], src[:, :, words])
 
         def transpose(k):
             unit = UNITS[k]
@@ -204,19 +208,17 @@ def tile_quadjetresnetblock_pb_kernel(tc, x, q2, q1, W3, b3, out):
                 tag = "product%d" % h
                 bank = psum.tile([P, K_PASS], F32, name=tag, tag=tag)
                 nc.tensor.matmul(out=bank[:], lhsT=ones[:], rhs=bias_row[:, cols], start=True, stop=True)
-                nc.vector.tensor_copy(out=bias[:, cols], in_=bank[:])
+                nc.scalar.copy(out=bias[:, cols], in_=bank[:])
 
         ready, waiting, multiplied, added = set(), [], [], []
         step = 0
         while step < len(UNITS) + 2 or waiting or multiplied or added:
             if step < len(UNITS):
                 set_taps_apart(step)
-            if step == 2:
+            if step == 0:
                 spread_bias()
             if 0 <= step - 1 < len(UNITS):
                 transpose(step - 1)
-            for i, j in added:
-                relu_and_store(i, j)
             now, waiting = waiting[:PRODUCTS_A_STEP], waiting[PRODUCTS_A_STEP:]
             for i, j in now:
                 multiply(i, j)
@@ -228,10 +230,12 @@ def tile_quadjetresnetblock_pb_kernel(tc, x, q2, q1, W3, b3, out):
                         needs = {("q2", i, 0), ("x", i, 0), ("x", i, 1), ("w", j, 0)}
                         if needs <= ready and UNITS[step - 2] in needs:
                             waiting.append((i, j))
-            if 0 <= step - 1 < len(UNITS):
-                regroup(step - 1)
             if 0 <= step - FIRST_RESIDUAL_STEP < W_TILES:
                 residual_plus_bias(step - FIRST_RESIDUAL_STEP)
+            if 0 <= step - 1 < len(UNITS):
+                regroup(step - 1)
+            for i, j in added:
+                relu_and_store(i, j)
             for i, j in multiplied:
                 add_product(i, j)
             added, multiplied = multiplied, now

@@ -24,15 +24,14 @@ FLOPS = 2 * N_ROWS * GROUPS * CHANNELS * CHANNELS * TAPS
 
 UNITS = (
     [("q2", i, 0) for i in range(ROW_TILES)]
-    + [("x", 0, h) for h in range(HALVES)]
     + [("w", 0, 0)]
-    + [("x", 1, h) for h in range(HALVES)]
+    + [("x", i, h) for i in range(ROW_TILES) for h in range(HALVES)]
     + [("w", j, 0) for j in range(1, W_TILES)]
 )
 LOADS_BEFORE_RESIDUAL = 8
 FIRST_RESIDUAL_STEP = 8
 PRODUCTS_A_STEP = 3
-VECTOR_COLS = 416
+VECTOR_COLS = 480
 LATE_W, LATE_VECTOR_COLS = 3, 256
 COPY_BUFS = 3
 GROUPED_BUFS = 3
@@ -145,7 +144,7 @@ def tile_quadjetresnetblock_pb_kernel(tc, x, q2, q1, W3, b3, out):
                     )
                 else:
                     copy(
-                        k % 2 == 0 and b == BANKS - 1,
+                        False,
                         dst.rearrange("p (h r u) -> p h r u", h=2, u=2),
                         bank.rearrange("p (h u) r -> p h r u", u=2),
                     )
@@ -197,7 +196,10 @@ def tile_quadjetresnetblock_pb_kernel(tc, x, q2, q1, W3, b3, out):
             nc.vector.tensor_tensor(out=view, in0=product[(i, j)][:].rearrange("p g o -> p o g"), in1=view, op=ADD)
 
         def relu_and_store(i, j):
-            nc.scalar.activation(out=result[j][:, i, :], in_=result[j][:, i, :], func=RELU)
+            if i == 1:
+                nc.vector.tensor_scalar_max(out=result[j][:, i, :], in0=result[j][:, i, :], scalar1=0.0)
+            else:
+                nc.scalar.activation(out=result[j][:, i, :], in_=result[j][:, i, :], func=RELU)
             nc.sync.dma_start(
                 out=out[rows(i), P * j:P * (j + 1), :].rearrange("n o g -> n (o g)"), in_=result[j][:, i, :]
             )

@@ -53,6 +53,8 @@ def tile_quadjetresnetblock_pb_kernel(tc, x, q2, q1, W3, b3, out):
         nc.gpsimd.memset(ones[:], 1.0)
         identity = fixed.tile([P, P], F32, name="identity")
         make_identity(nc, identity[:])
+        identity_bf16 = fixed.tile([P, P], BF16, name="identity_bf16")
+        make_identity(nc, identity_bf16[:])
         bias = fixed.tile([P, CHANNELS], BF16, name="bias")
         loaded, codes, scales = {}, {}, {}
         for unit in UNITS:
@@ -116,18 +118,25 @@ def tile_quadjetresnetblock_pb_kernel(tc, x, q2, q1, W3, b3, out):
             transposed[k] = []
             for b in range(BANKS):
                 tag = "transposed%d" % ((BANKS * k + b) % TRANSPOSE_BANKS)
-                bank = psum.tile([P, 4, P], F32, name=tag, tag=tag)
-                transposed[k].append(bank)
                 if unit[0] == "x":
-                    words = loaded[unit][:].bitcast(F32).rearrange("r (p u e g) -> r u e g p", u=2, e=2, g=GROUPS)
-                    for u in range(2):
-                        for e in range(2):
-                            nc.tensor.transpose(bank[:, 2 * u + e, :], words[:, u, e, b, :], identity[:])
+                    bank = psum.tile([P, 2, 4, P], BF16, name=tag, tag=tag)
+                    values = loaded[unit][:].rearrange("r (p v j) -> r j v p", v=4, j=SIXTHS)
+                    for t in range(2):
+                        for v in range(4):
+                            nc.tensor.matmul(
+                                out=bank[:, t, v, :],
+                                lhsT=values[:, 2 * b + t, v, :],
+                                rhs=identity_bf16[:],
+                                start=True,
+                                stop=True,
+                            )
                 else:
+                    bank = psum.tile([P, 4, P], F32, name=tag, tag=tag)
                     for h in range(HALVES):
                         for u in range(2):
                             run = apart[k][:, 2 * b + u, 256 * h:256 * (h + 1)]
                             nc.tensor.transpose(bank[:, 2 * h + u, :], run.bitcast(F32), identity[:])
+                transposed[k].append(bank)
 
         def regroup(k):
             unit = UNITS[k]
@@ -140,7 +149,7 @@ def tile_quadjetresnetblock_pb_kernel(tc, x, q2, q1, W3, b3, out):
                     copy(
                         b == 1,
                         dst.bitcast(BF16).rearrange("p (t r v) -> p t r v", t=2, v=4),
-                        bank.bitcast(BF16).rearrange("p v (r t) -> p t r v", t=2),
+                        bank.rearrange("p t v r -> p t r v"),
                     )
                 else:
                     copy(

from contextlib import ExitStack

import concourse.mybir as mybir
from concourse.masks import make_identity

FP8X4 = mybir.dt.float8_e4m3fn_x4
BF16 = mybir.dt.bfloat16
F32 = mybir.dt.float32
U32 = mybir.dt.uint32
U8 = mybir.dt.uint8
ADD = mybir.AluOpType.add
RELU = mybir.ActivationFunctionType.Relu

P = 128
N_ROWS, CHANNELS, GROUPS, TAPS = 256, 1024, 3, 3
ROW_TILES = N_ROWS // P
W_TILES = CHANNELS // P
K_PASS = 512
HALVES = CHANNELS // K_PASS
SIXTHS = 6
UNIT = SIXTHS * K_PASS
BANKS = 3
FLOPS = 2 * N_ROWS * GROUPS * CHANNELS * CHANNELS * TAPS

UNITS = (
    [("q2", i, 0) for i in range(ROW_TILES)]
    + [("w", 0, 0)]
    + [("x", i, h) for i in range(ROW_TILES) for h in range(HALVES)]
    + [("w", j, 0) for j in range(1, W_TILES)]
)
LOADS_BEFORE_RESIDUAL = 8
FIRST_RESIDUAL_STEP = 8
PRODUCTS_A_STEP = 3
VECTOR_COLS = 480
LATE_W, LATE_VECTOR_COLS = 3, 256
COPY_BUFS = 3
GROUPED_BUFS = 3
TRANSPOSE_BANKS = 4
PRODUCT_BANKS = 4


def tile_quadjetresnetblock_pb_kernel(tc, x, q2, q1, W3, b3, out):
    nc = tc.nc
    with ExitStack() as ctx:
        ctx.enter_context(tc.manual_schedule())
        fixed = ctx.enter_context(tc.tile_pool(name="fixed", bufs=1))
        rotating = ctx.enter_context(tc.tile_pool(name="rotating", bufs=1))
        psum = ctx.enter_context(tc.psum_pool(name="psum", bufs=1))

        bias_row = fixed.tile([P, CHANNELS], BF16, name="bias_row")
        nc.gpsimd.memset(bias_row[:], 0.0)
        ones = fixed.tile([P, P], BF16, name="ones")
        nc.gpsimd.memset(ones[:], 1.0)
        identity = fixed.tile([P, P], F32, name="identity")
        make_identity(nc, identity[:])
        identity_bf16 = fixed.tile([P, P], BF16, name="identity_bf16")
        make_identity(nc, identity_bf16[:])
        bias = fixed.tile([P, CHANNELS], BF16, name="bias")
        loaded, codes, scales = {}, {}, {}
        for unit in UNITS:
            loaded[unit] = fixed.tile([P, UNIT], BF16, name="loaded_%s%d%d" % unit)
            codes[unit] = fixed.tile([P, UNIT // 4], U32, name="codes_%s%d%d" % unit, align_bytes=64)
            scales[unit] = fixed.tile([P, UNIT // 4], U8, name="scales_%s%d%d" % unit, align_bytes=64)
        q1_loaded = fixed.tile([P, ROW_TILES, GROUPS * CHANNELS], BF16, name="q1_loaded")
        result = [fixed.tile([P, ROW_TILES, GROUPS * P], F32, name="result%d" % j) for j in range(W_TILES)]

        def rows(i):
            return slice(P * i, P * (i + 1))

        for k, unit in enumerate(UNITS):
            kind, i, h = unit
            if k == LOADS_BEFORE_RESIDUAL:
                for r in range(ROW_TILES):
                    nc.sync.dma_start(out=q1_loaded[:, r, :], in_=q1[rows(r), :, :].rearrange("n o g -> n (o g)"))
            if kind == "x":
                source = x[rows(i), K_PASS * h:K_PASS * (h + 1), :].rearrange("n c j -> n (c j)")
            elif kind == "q2":
                source = q2[rows(i), :, :].rearrange("n c g -> n (c g)")
            else:
                source = W3[rows(i), :, :].rearrange("o c t -> o (c t)")
            if k == 0:
                for half in range(HALVES):
                    cols = slice(UNIT // 2 * half, UNIT // 2 * (half + 1))
                    nc.sync.dma_start(out=loaded[unit][:, cols], in_=source[:, cols])
                    if half == 0:
                        nc.sync.dma_start(out=bias_row[0:1, :], in_=b3.rearrange("(a o) -> a o", a=1))
            else:
                nc.sync.dma_start(out=loaded[unit][:], in_=source)

        apart, transposed, grouped, product = {}, {}, {}, {}

        def copy(on_vector, dst, src):
            if on_vector:
                nc.vector.tensor_copy(out=dst, in_=src)
            else:
                nc.scalar.copy(out=dst, in_=src)

        def set_taps_apart(k):
            unit = UNITS[k]
            if unit[0] == "x":
                return
            tag = "apart%d" % (k % COPY_BUFS)
            apart[k] = rotating.tile([P, SIXTHS, K_PASS], BF16, name=tag, tag=tag)
            src = loaded[unit][:].rearrange("p (m u e t) -> p t m u e", u=2, e=2, t=TAPS)
            dst = apart[k][:].rearrange("p (t u) (m e) -> p t m u e", u=2, e=2)
            parts = HALVES if k == 0 else 1
            for part in range(parts):
                start, width = K_PASS // parts * part, K_PASS // parts
                cut = start + (LATE_VECTOR_COLS if unit[0] == "w" and unit[1] >= LATE_W else VECTOR_COLS) // parts
                words = slice(start // 2, cut // 2)
                copy(True, dst[:, 0:2, words], src[:, 0:2, words])
                copy(True, dst[:, 2, words], src[:, 2, words])
                words = slice(cut // 2, (start + width) // 2)
                copy(False, dst[:, :, words], src[:, :, words])

        def transpose(k):
            unit = UNITS[k]
            transposed[k] = []
            for b in range(BANKS):
                tag = "transposed%d" % ((BANKS * k + b) % TRANSPOSE_BANKS)
                if unit[0] == "x":
                    bank = psum.tile([P, 2, 4, P], BF16, name=tag, tag=tag)
                    values = loaded[unit][:].rearrange("r (p v j) -> r j v p", v=4, j=SIXTHS)
                    for t in range(2):
                        for v in range(4):
                            nc.tensor.matmul(
                                out=bank[:, t, v, :],
                                lhsT=values[:, 2 * b + t, v, :],
                                rhs=identity_bf16[:],
                                start=True,
                                stop=True,
                            )
                else:
                    bank = psum.tile([P, 4, P], F32, name=tag, tag=tag)
                    for h in range(HALVES):
                        for u in range(2):
                            run = apart[k][:, 2 * b + u, 256 * h:256 * (h + 1)]
                            nc.tensor.transpose(bank[:, 2 * h + u, :], run.bitcast(F32), identity[:])
                transposed[k].append(bank)

        def regroup(k):
            unit = UNITS[k]
            tag = "grouped%d" % (k % GROUPED_BUFS)
            grouped[k] = rotating.tile([P, UNIT // 2], F32, name=tag, tag=tag, align_bytes=64)
            for b in range(BANKS):
                dst = grouped[k][:, 512 * b:512 * (b + 1)]
                bank = transposed[k][b][:]
                if unit[0] == "x":
                    copy(
                        b == 1,
                        dst.bitcast(BF16).rearrange("p (t r v) -> p t r v", t=2, v=4),
                        bank.rearrange("p t v r -> p t r v"),
                    )
                else:
                    copy(
                        False,
                        dst.rearrange("p (h r u) -> p h r u", h=2, u=2),
                        bank.rearrange("p (h u) r -> p h r u", u=2),
                    )

        def quantise(k):
            unit = UNITS[k]
            for lo, hi in ((0, 512), (512, 768)):
                nc.vector.quantize_mx(
                    out=codes[unit][:, lo:hi].bitcast(FP8X4),
                    scales=scales[unit][:, lo:hi],
                    in_=grouped[k][:, 2 * lo:2 * hi].bitcast(BF16),
                )

        def operand(unit, sixth):
            cols = slice(P * sixth, P * (sixth + 1))
            return codes[unit][:, cols].bitcast(FP8X4), scales[unit][:, cols]

        def multiply(i, j):
            tag = "product%d" % (len(product) % PRODUCT_BANKS)
            product[(i, j)] = psum.tile([P, GROUPS, P], F32, name=tag, tag=tag)
            passes = [(t, h) for t in range(TAPS) for h in range(HALVES)]
            for g in range(GROUPS):
                for t, h in passes:
                    if t < 2:
                        a_codes, a_scales = operand(("x", i, h), 2 * g + t)
                    else:
                        a_codes, a_scales = operand(("q2", i, 0), HALVES * g + h)
                    w_codes, w_scales = operand(("w", j, 0), HALVES * t + h)
                    nc.tensor.matmul_mx(
                        out=product[(i, j)][:, g, :],
                        lhsT=a_codes,
                        lhsT_scale=a_scales,
                        rhs=w_codes,
                        rhs_scale=w_scales,
                        start=(t, h) == passes[0],
                        stop=(t, h) == passes[-1],
                    )

        def residual_plus_bias(j):
            nc.vector.tensor_tensor(
                out=result[j][:].rearrange("p i (o g) -> p i o g", g=GROUPS),
                in0=q1_loaded[:, :, GROUPS * P * j:GROUPS * P * (j + 1)].rearrange("p i (o g) -> p i o g", g=GROUPS),
                in1=bias[:, P * j:P * (j + 1)].unsqueeze(1).unsqueeze(3).to_broadcast([P, ROW_TILES, P, GROUPS]),
                op=ADD,
            )

        def add_product(i, j):
            view = result[j][:, i, :].rearrange("p (o g) -> p o g", g=GROUPS)
            nc.vector.tensor_tensor(out=view, in0=product[(i, j)][:].rearrange("p g o -> p o g"), in1=view, op=ADD)

        def relu_and_store(i, j):
            if i == 1:
                nc.vector.tensor_scalar_max(out=result[j][:, i, :], in0=result[j][:, i, :], scalar1=0.0)
            else:
                nc.scalar.activation(out=result[j][:, i, :], in_=result[j][:, i, :], func=RELU)
            nc.sync.dma_start(
                out=out[rows(i), P * j:P * (j + 1), :].rearrange("n o g -> n (o g)"), in_=result[j][:, i, :]
            )

        def spread_bias():
            for h in range(HALVES):
                cols = slice(K_PASS * h, K_PASS * (h + 1))
                tag = "product%d" % h
                bank = psum.tile([P, K_PASS], F32, name=tag, tag=tag)
                nc.tensor.matmul(out=bank[:], lhsT=ones[:], rhs=bias_row[:, cols], start=True, stop=True)
                nc.scalar.copy(out=bias[:, cols], in_=bank[:])

        ready, waiting, multiplied, added = set(), [], [], []
        step = 0
        while step < len(UNITS) + 2 or waiting or multiplied or added:
            if step < len(UNITS):
                set_taps_apart(step)
            if step == 0:
                spread_bias()
            if 0 <= step - 1 < len(UNITS):
                transpose(step - 1)
            now, waiting = waiting[:PRODUCTS_A_STEP], waiting[PRODUCTS_A_STEP:]
            for i, j in now:
                multiply(i, j)
            if 0 <= step - 2 < len(UNITS):
                quantise(step - 2)
                ready.add(UNITS[step - 2])
                for j in range(W_TILES):
                    for i in range(ROW_TILES):
                        needs = {("q2", i, 0), ("x", i, 0), ("x", i, 1), ("w", j, 0)}
                        if needs <= ready and UNITS[step - 2] in needs:
                            waiting.append((i, j))
            if 0 <= step - FIRST_RESIDUAL_STEP < W_TILES:
                residual_plus_bias(step - FIRST_RESIDUAL_STEP)
            if 0 <= step - 1 < len(UNITS):
                regroup(step - 1)
            for i, j in added:
                relu_and_store(i, j)
            for i, j in multiplied:
                add_product(i, j)
            added, multiplied = multiplied, now
            step += 1
